import numpy as np
import ml_dtypes


def mxq(x, axis, fmt="e4m3"):
    dtype, down = {"e4m3": (ml_dtypes.float8_e4m3fn, 7), "e5m2": (ml_dtypes.float8_e5m2, 14)}[fmt]
    v = np.moveaxis(np.asarray(x, np.float32).astype(ml_dtypes.bfloat16).astype(np.float64), axis, -1)
    blocks = v.reshape(v.shape[:-1] + (-1, 32))
    amax = np.abs(blocks).max(-1, keepdims=True)
    byte = np.maximum(np.where(amax > 0, np.frexp(amax)[1] - 1 + 127, 0) - down, 1)
    scale = np.exp2(byte - 127.0)
    codes = (blocks / scale).astype(np.float32).astype(dtype).astype(np.float64)
    return np.moveaxis((codes * scale).reshape(v.shape), -1, axis)


WIDE = False


def mx_kscale(k):
    if not WIDE:
        return np.ones(k)
    levels = np.array([10, -10, 5, -5, 0])
    if k % 512:
        return np.exp2(np.random.permutation(np.resize(levels, k // 32))).repeat(32)
    a = np.empty((k // 512, 16))
    for p in range(k // 512):
        a[p, :8] = np.random.permutation(np.resize(levels, 8))
        for g in range(8):
            far = levels[np.abs(levels - a[p, g]) >= 10]
            a[p, g + 8] = far[np.random.randint(len(far))]
    return np.exp2(a.ravel()).repeat(32)


BF16 = ml_dtypes.bfloat16


def bf(x):
    return np.asarray(x, np.float32).astype(BF16)


def f64(x):
    return np.asarray(x).astype(np.float64)


B, D_IN, D_FEAT, N_EX, N_LAB = 1024, 512, 512, 8192, 128
EPS = 1e-12


def l2_normalize(x):
    n = np.sqrt((x * x).sum(-1, keepdims=True))
    return x / np.maximum(n, EPS)


def setup_inputs():
    s = mx_kscale(D_IN)
    return {"features": bf(np.random.standard_normal((B, D_IN)) * s),
            "ex_features": bf(np.random.standard_normal((N_EX, D_IN)) * s),
            "g_weight": bf(np.random.standard_normal((D_FEAT, D_IN)) / np.sqrt(D_IN) / s)}


def reference(features, ex_features, g_weight):
    gq = mxq(f64(g_weight), 1, "e4m3")
    f = mxq(f64(features), 1, "e4m3") @ gq.T
    e = mxq(f64(ex_features), 1, "e4m3") @ gq.T
    return l2_normalize(f), l2_normalize(e)

@@ -1,0 +1,198 @@
+from contextlib import ExitStack
+
+import concourse.mybir as mybir
+from concourse.masks import make_identity
+
+F32 = mybir.dt.float32
+BF16 = mybir.dt.bfloat16
+U32 = mybir.dt.uint32
+U8 = mybir.dt.uint8
+FP8X4 = mybir.dt.float8_e4m3fn_x4
+ACT = mybir.ActivationFunctionType
+ALU = mybir.AluOpType
+
+P = 128
+K = 512
+N = 512
+WORDS = K // 2
+UNIT = 2
+G_UNITS = N // (UNIT * P)
+GROUP = 8
+STORE_TILES = 4
+PSUM_BANKS = 8
+FLIP_BANKS = 2
+PRODUCT_BANKS = PSUM_BANKS - FLIP_BANKS
+FRONT_LEAD = G_UNITS + 4
+VECTOR_COPIES_EVERY = 4
+EPS = 1e-12
+
+FLOPS = 2 * (1024 + 8192) * K * N
+
+
+def tile_minerva_pb_kernel(tc, features, ex_features, g_weight, out_0, out_1):
+    nc = tc.nc
+    row_tiles = (features.shape[0] + ex_features.shape[0]) // P
+    pairs = row_tiles // UNIT
+    with ExitStack() as ctx:
+        const = ctx.enter_context(tc.tile_pool(name="const", bufs=1))
+        rows_pool = ctx.enter_context(tc.tile_pool(name="rows", bufs=1))
+        grouped_pool = ctx.enter_context(tc.tile_pool(name="grouped", bufs=3))
+        norm_pool = ctx.enter_context(tc.tile_pool(name="norms", bufs=3))
+        result_pool = ctx.enter_context(tc.tile_pool(name="result", bufs=8))
+        psum = ctx.enter_context(tc.psum_pool(name="psum", bufs=1))
+        ctx.enter_context(tc.manual_schedule())
+
+        g_rows = const.tile([P, G_UNITS * UNIT * K], BF16, name="g_rows")
+        g_src = g_weight.rearrange("(t p) k -> p t k", p=P)
+        g_dst = g_rows[:].rearrange("p (t k) -> p t k", k=K)
+        for b in range(G_UNITS):
+            tiles = slice(b * UNIT, (b + 1) * UNIT)
+            nc.sync.dma_start(out=g_dst[:, tiles, :], in_=g_src[:, tiles, :])
+        x_words = []
+        out_views = []
+        for x, out in ((features, out_0), (ex_features, out_1)):
+            for base in range(0, x.shape[0], GROUP * P):
+                x_rows = rows_pool.tile([P, GROUP * K], BF16, name="x_rows%d" % len(out_views))
+                src = x[base : base + GROUP * P, :].rearrange("(p t) k -> p (t k)", t=GROUP)
+                pieces = GROUP // UNIT if len(out_views) == 0 else 1
+                width = GROUP * K // pieces
+                for c in range(pieces):
+                    cols = slice(c * width, (c + 1) * width)
+                    nc.sync.dma_start(out=x_rows[:, cols], in_=src[:, cols])
+                words = x_rows[:].bitcast(F32)
+                for c in range(GROUP // UNIT):
+                    x_words.append(words[:, c * UNIT * WORDS : (c + 1) * UNIT * WORDS])
+                out_views.append(
+                    out[base : base + GROUP * P, :].rearrange("(p t) n -> p t n", t=GROUP)
+                )
+
+        identity = const.tile([P, P], F32, name="identity")
+        make_identity(nc, identity[:])
+
+        minus_half = const.tile([P, UNIT], F32, name="minus_half")
+        nc.vector.memset(minus_half[:], -0.5)
+
+        g_codes = const.tile([P, N], U32, align_bytes=64, name="g_codes")
+        g_scales = const.tile([P, N], U8, align_bytes=64, name="g_scales")
+        x_codes = const.tile([P, row_tiles * P], U32, align_bytes=64, name="x_codes")
+        x_scales = const.tile([P, row_tiles * P], U8, align_bytes=64, name="x_scales")
+
+        g_words = g_rows[:].bitcast(F32)
+        units = []
+        for b in range(G_UNITS):
+            cols = slice(b * UNIT * P, (b + 1) * UNIT * P)
+            words = g_words[:, b * UNIT * WORDS : (b + 1) * UNIT * WORDS]
+            units.append((words, g_codes[:, cols], g_scales[:, cols]))
+        for pair in range(pairs):
+            cols = slice(pair * UNIT * P, (pair + 1) * UNIT * P)
+            units.append((x_words[pair], x_codes[:, cols], x_scales[:, cols]))
+
+        flipped_of = {}
+        grouped_of = {}
+
+        def transpose(u):
+            bank = u if u < PRODUCT_BANKS else PRODUCT_BANKS + u % FLIP_BANKS
+            flipped = psum.tile([P, UNIT, 2, P], F32, name="flipped", tag="bank%d" % bank)
+            words = units[u][0]
+            for j in range(UNIT):
+                for h in range(2):
+                    every_2nd = slice(j * WORDS + h, (j + 1) * WORDS, 2)
+                    nc.tensor.transpose(flipped[:, j, h, :], words[:, every_2nd], identity[:])
+            flipped_of[u] = flipped
+
+        def copy_out(u):
+            grouped = grouped_pool.tile([P, UNIT * K], BF16, align_bytes=64, name="grouped")
+            dst = grouped[:].bitcast(F32).rearrange("p (j row h) -> p j row h", j=UNIT, h=2)
+            src = flipped_of[u][:].rearrange("p j h row -> p j row h")
+            if u % VECTOR_COPIES_EVERY == 0:
+                nc.vector.tensor_copy(out=dst, in_=src)
+            else:
+                nc.scalar.copy(out=dst, in_=src)
+            grouped_of[u] = grouped
+
+        def quantise(u):
+            nc.vector.quantize_mx(
+                out=units[u][1].bitcast(FP8X4), scales=units[u][2], in_=grouped_of[u][:]
+            )
+
+        def front(u):
+            if u < len(units):
+                transpose(u)
+            if 0 <= u - 1 < len(units):
+                copy_out(u - 1)
+            if 0 <= u - 2 < len(units):
+                quantise(u - 2)
+
+        products_of = {}
+        result_of = {}
+        inverse_of = {}
+
+        def multiply(pair):
+            products_of[pair] = []
+            for j in range(UNIT):
+                t = pair * UNIT + j
+                acc = psum.tile([P, N], F32, name="acc", tag="bank%d" % (t % PRODUCT_BANKS))
+                nc.tensor.matmul_mx(
+                    out=acc[:],
+                    lhsT=x_codes[:, t * P : (t + 1) * P].bitcast(FP8X4),
+                    lhsT_scale=x_scales[:, t * P : (t + 1) * P],
+                    rhs=g_codes[:].bitcast(FP8X4),
+                    rhs_scale=g_scales[:],
+                    start=True,
+                    stop=True,
+                )
+                products_of[pair].append(acc)
+
+        def inverse_norms(pair):
+            if pair * UNIT % STORE_TILES == 0:
+                result = result_pool.tile([P, STORE_TILES, N], F32, name="result")
+                result_of[pair * UNIT // STORE_TILES] = result
+            sumsq = norm_pool.tile([P, UNIT], F32, name="sumsq")
+            for j in range(UNIT):
+                t = pair * UNIT + j
+                nc.scalar.activation(
+                    out=result_of[t // STORE_TILES][:, t % STORE_TILES, :],
+                    in_=products_of[pair][j][:],
+                    func=ACT.Square,
+                    accum_out=sumsq[:, j : j + 1],
+                )
+            floored = norm_pool.tile([P, UNIT], F32, name="floored")
+            nc.gpsimd.tensor_scalar(
+                out=floored[:], in0=sumsq[:], scalar1=EPS * EPS, scalar2=None, op0=ALU.max
+            )
+            inverse = norm_pool.tile([P, UNIT], F32, name="inverse")
+            nc.gpsimd.tensor_tensor(out=inverse[:], in0=floored[:], in1=minus_half[:], op=ALU.pow)
+            inverse_of[pair] = inverse
+
+        def scale_and_store(pair):
+            for j in range(UNIT):
+                t = pair * UNIT + j
+                nc.vector.tensor_scalar(
+                    out=result_of[t // STORE_TILES][:, t % STORE_TILES, :],
+                    in0=products_of[pair][j][:],
+                    scalar1=inverse_of[pair][:, j : j + 1],
+                    scalar2=None,
+                    op0=ALU.mult,
+                )
+            done = (pair + 1) * UNIT
+            in_last_store = done > row_tiles - STORE_TILES
+            if in_last_store or done % STORE_TILES == 0:
+                count = UNIT if in_last_store else STORE_TILES
+                first = done - count
+                nc.sync.dma_start(
+                    out=out_views[first // GROUP][:, first % GROUP : first % GROUP + count, :],
+                    in_=result_of[first // STORE_TILES][
+                        :, first % STORE_TILES : first % STORE_TILES + count, :
+                    ],
+                )
+
+        for u in range(FRONT_LEAD):
+            front(u)
+        for i in range(pairs + 2):
+            if 0 <= i - 2:
+                scale_and_store(i - 2)
+            if i < pairs:
+                multiply(i)
+            if 0 <= i - 1 < pairs:
+                inverse_norms(i - 1)
+            front(FRONT_LEAD + i)

@@ -66,11 +66,13 @@ def tile_minerva_pb_kernel(tc, features, ex_features, g_weight, out_0, out_1):
                     out[base : base + GROUP * P, :].rearrange("(p t) n -> p t n", t=GROUP)
                 )
 
+        one = const.tile([P, 1], F32, name="one")
+        nc.vector.memset(one[:], 1.0)
+        table_loaded = const.tile([P, 1], F32, name="table_loaded")
+        nc.scalar.activation(out=table_loaded[:], in_=one[:], func=ACT.Abs_reciprocal_sqrt)
+
         identity = const.tile([P, P], F32, name="identity")
         make_identity(nc, identity[:])
-
-        minus_half = const.tile([P, UNIT], F32, name="minus_half")
-        nc.vector.memset(minus_half[:], -0.5)
 
         g_codes = const.tile([P, N], U32, align_bytes=64, name="g_codes")
         g_scales = const.tile([P, N], U8, align_bytes=64, name="g_scales")
@@ -125,6 +127,7 @@ def tile_minerva_pb_kernel(tc, features, ex_features, g_weight, out_0, out_1):
 
         products_of = {}
         result_of = {}
+        floored_of = {}
         inverse_of = {}
 
         def multiply(pair):
@@ -156,12 +159,19 @@ def tile_minerva_pb_kernel(tc, features, ex_features, g_weight, out_0, out_1):
                     func=ACT.Square,
                     accum_out=sumsq[:, j : j + 1],
                 )
+                if j == 0 and 0 <= pair - 1:
+                    invert(pair - 1)
             floored = norm_pool.tile([P, UNIT], F32, name="floored")
             nc.gpsimd.tensor_scalar(
                 out=floored[:], in0=sumsq[:], scalar1=EPS * EPS, scalar2=None, op0=ALU.max
             )
+            floored_of[pair] = floored
+
+        def invert(pair):
             inverse = norm_pool.tile([P, UNIT], F32, name="inverse")
-            nc.gpsimd.tensor_tensor(out=inverse[:], in0=floored[:], in1=minus_half[:], op=ALU.pow)
+            nc.scalar.activation(
+                out=inverse[:], in_=floored_of[pair][:], func=ACT.Abs_reciprocal_sqrt
+            )
             inverse_of[pair] = inverse
 
         def scale_and_store(pair):
@@ -189,10 +199,12 @@ def tile_minerva_pb_kernel(tc, features, ex_features, g_weight, out_0, out_1):
         for u in range(FRONT_LEAD):
             front(u)
         for i in range(pairs + 2):
-            if 0 <= i - 2:
-                scale_and_store(i - 2)
             if i < pairs:
                 multiply(i)
             if 0 <= i - 1 < pairs:
                 inverse_norms(i - 1)
+            if i - 1 == pairs:
+                invert(pairs - 1)
+            if 0 <= i - 2:
+                scale_and_store(i - 2)
             front(FRONT_LEAD + i)

@@ -18,12 +18,12 @@ WORDS = K // 2
 UNIT = 2
 G_UNITS = N // (UNIT * P)
 GROUP = 8
-STORE_TILES = 4
+STORE_TILES = 2
 PSUM_BANKS = 8
 FLIP_BANKS = 2
 PRODUCT_BANKS = PSUM_BANKS - FLIP_BANKS
 FRONT_LEAD = G_UNITS + 4
-VECTOR_COPIES_EVERY = 4
+VECTOR_COPIES_EVERY = 3
 EPS = 1e-12
 
 FLOPS = 2 * (1024 + 8192) * K * N
@@ -38,7 +38,7 @@ def tile_minerva_pb_kernel(tc, features, ex_features, g_weight, out_0, out_1):
         rows_pool = ctx.enter_context(tc.tile_pool(name="rows", bufs=1))
         grouped_pool = ctx.enter_context(tc.tile_pool(name="grouped", bufs=3))
         norm_pool = ctx.enter_context(tc.tile_pool(name="norms", bufs=3))
-        result_pool = ctx.enter_context(tc.tile_pool(name="result", bufs=8))
+        result_pool = ctx.enter_context(tc.tile_pool(name="result", bufs=16))
         psum = ctx.enter_context(tc.psum_pool(name="psum", bufs=1))
         ctx.enter_context(tc.manual_schedule())
 
@@ -151,6 +151,7 @@ def tile_minerva_pb_kernel(tc, features, ex_features, g_weight, out_0, out_1):
                 result = result_pool.tile([P, STORE_TILES, N], F32, name="result")
                 result_of[pair * UNIT // STORE_TILES] = result
             sumsq = norm_pool.tile([P, UNIT], F32, name="sumsq")
+            floored = norm_pool.tile([P, UNIT], F32, name="floored")
             for j in range(UNIT):
                 t = pair * UNIT + j
                 nc.scalar.activation(
@@ -159,42 +160,51 @@ def tile_minerva_pb_kernel(tc, features, ex_features, g_weight, out_0, out_1):
                     func=ACT.Square,
                     accum_out=sumsq[:, j : j + 1],
                 )
+                if pair == pairs - 1 or j == UNIT - 1:
+                    fresh = slice(j if pair == pairs - 1 else 0, j + 1)
+                    nc.gpsimd.tensor_scalar(
+                        out=floored[:, fresh],
+                        in0=sumsq[:, fresh],
+                        scalar1=EPS * EPS,
+                        scalar2=None,
+                        op0=ALU.max,
+                    )
                 if j == 0 and 0 <= pair - 1:
                     invert(pair - 1)
-            floored = norm_pool.tile([P, UNIT], F32, name="floored")
-            nc.gpsimd.tensor_scalar(
-                out=floored[:], in0=sumsq[:], scalar1=EPS * EPS, scalar2=None, op0=ALU.max
-            )
             floored_of[pair] = floored
 
         def invert(pair):
             inverse = norm_pool.tile([P, UNIT], F32, name="inverse")
-            nc.scalar.activation(
-                out=inverse[:], in_=floored_of[pair][:], func=ACT.Abs_reciprocal_sqrt
-            )
+            width = 1 if pair == pairs - 1 else UNIT
+            for j in range(0, UNIT, width):
+                nc.scalar.activation(
+                    out=inverse[:, j : j + width],
+                    in_=floored_of[pair][:, j : j + width],
+                    func=ACT.Abs_reciprocal_sqrt,
+                )
             inverse_of[pair] = inverse
 
         def scale_and_store(pair):
             for j in range(UNIT):
                 t = pair * UNIT + j
-                nc.vector.tensor_scalar(
-                    out=result_of[t // STORE_TILES][:, t % STORE_TILES, :],
-                    in0=products_of[pair][j][:],
-                    scalar1=inverse_of[pair][:, j : j + 1],
-                    scalar2=None,
-                    op0=ALU.mult,
-                )
-            done = (pair + 1) * UNIT
-            in_last_store = done > row_tiles - STORE_TILES
-            if in_last_store or done % STORE_TILES == 0:
-                count = UNIT if in_last_store else STORE_TILES
-                first = done - count
-                nc.sync.dma_start(
-                    out=out_views[first // GROUP][:, first % GROUP : first % GROUP + count, :],
-                    in_=result_of[first // STORE_TILES][
-                        :, first % STORE_TILES : first % STORE_TILES + count, :
-                    ],
-                )
+                result = result_of[t // STORE_TILES][:, t % STORE_TILES, :]
+                product = products_of[pair][j][:]
+                inverse = inverse_of[pair][:, j : j + 1]
+                if t == row_tiles - 1:
+                    nc.scalar.activation(out=result, in_=product, func=ACT.Copy, scale=inverse)
+                else:
+                    nc.vector.tensor_scalar(
+                        out=result, in0=product, scalar1=inverse, scalar2=None, op0=ALU.mult
+                    )
+                count = 1 if pair == pairs - 1 else STORE_TILES
+                if (t + 1) % count == 0:
+                    first = t + 1 - count
+                    nc.sync.dma_start(
+                        out=out_views[first // GROUP][:, first % GROUP : first % GROUP + count, :],
+                        in_=result_of[first // STORE_TILES][
+                            :, first % STORE_TILES : first % STORE_TILES + count, :
+                        ],
+                    )
 
         for u in range(FRONT_LEAD):
             front(u)

@@ -16,14 +16,16 @@ K = 512
 N = 512
 WORDS = K // 2
 UNIT = 2
-G_UNITS = N // (UNIT * P)
+G_UNITS = N // P
 GROUP = 8
 STORE_TILES = 2
 PSUM_BANKS = 8
 FLIP_BANKS = 2
 PRODUCT_BANKS = PSUM_BANKS - FLIP_BANKS
 FRONT_LEAD = G_UNITS + 4
-VECTOR_COPIES_EVERY = 3
+WARM_UPS = 12
+COPY_CYCLE = 5
+VECTOR_COPIES = (1, 3)
 EPS = 1e-12
 
 FLOPS = 2 * (1024 + 8192) * K * N
@@ -42,19 +44,17 @@ def tile_minerva_pb_kernel(tc, features, ex_features, g_weight, out_0, out_1):
         psum = ctx.enter_context(tc.psum_pool(name="psum", bufs=1))
         ctx.enter_context(tc.manual_schedule())
 
-        g_rows = const.tile([P, G_UNITS * UNIT * K], BF16, name="g_rows")
+        g_rows = const.tile([P, G_UNITS * K], BF16, name="g_rows")
         g_src = g_weight.rearrange("(t p) k -> p t k", p=P)
-        g_dst = g_rows[:].rearrange("p (t k) -> p t k", k=K)
         for b in range(G_UNITS):
-            tiles = slice(b * UNIT, (b + 1) * UNIT)
-            nc.sync.dma_start(out=g_dst[:, tiles, :], in_=g_src[:, tiles, :])
+            nc.sync.dma_start(out=g_rows[:, b * K : (b + 1) * K], in_=g_src[:, b, :])
         x_words = []
         out_views = []
         for x, out in ((features, out_0), (ex_features, out_1)):
             for base in range(0, x.shape[0], GROUP * P):
                 x_rows = rows_pool.tile([P, GROUP * K], BF16, name="x_rows%d" % len(out_views))
                 src = x[base : base + GROUP * P, :].rearrange("(p t) k -> p (t k)", t=GROUP)
-                pieces = GROUP // UNIT if len(out_views) == 0 else 1
+                pieces = GROUP // UNIT if len(out_views) < 2 else 1
                 width = GROUP * K // pieces
                 for c in range(pieces):
                     cols = slice(c * width, (c + 1) * width)
@@ -65,6 +65,14 @@ def tile_minerva_pb_kernel(tc, features, ex_features, g_weight, out_0, out_1):
                 out_views.append(
                     out[base : base + GROUP * P, :].rearrange("(p t) n -> p t n", t=GROUP)
                 )
+
+        zeros = const.tile([P, P], BF16, name="zeros")
+        nc.vector.memset(zeros[:], 0.0)
+        idle = psum.tile([P, P], F32, name="idle", tag="bank%d" % (PSUM_BANKS - 1))
+        for turn in range(WARM_UPS):
+            nc.tensor.matmul(
+                idle[:], lhsT=zeros[:], rhs=zeros[:], start=turn == 0, stop=turn == WARM_UPS - 1
+            )
 
         one = const.tile([P, 1], F32, name="one")
         nc.vector.memset(one[:], 1.0)
@@ -82,39 +90,41 @@ def tile_minerva_pb_kernel(tc, features, ex_features, g_weight, out_0, out_1):
         g_words = g_rows[:].bitcast(F32)
         units = []
         for b in range(G_UNITS):
-            cols = slice(b * UNIT * P, (b + 1) * UNIT * P)
-            words = g_words[:, b * UNIT * WORDS : (b + 1) * UNIT * WORDS]
-            units.append((words, g_codes[:, cols], g_scales[:, cols]))
+            cols = slice(b * P, (b + 1) * P)
+            words = g_words[:, b * WORDS : (b + 1) * WORDS]
+            units.append((1, words, g_codes[:, cols], g_scales[:, cols]))
         for pair in range(pairs):
             cols = slice(pair * UNIT * P, (pair + 1) * UNIT * P)
-            units.append((x_words[pair], x_codes[:, cols], x_scales[:, cols]))
+            units.append((UNIT, x_words[pair], x_codes[:, cols], x_scales[:, cols]))
 
         flipped_of = {}
         grouped_of = {}
 
         def transpose(u):
             bank = u if u < PRODUCT_BANKS else PRODUCT_BANKS + u % FLIP_BANKS
-            flipped = psum.tile([P, UNIT, 2, P], F32, name="flipped", tag="bank%d" % bank)
-            words = units[u][0]
-            for j in range(UNIT):
+            tiles, words = units[u][:2]
+            flipped = psum.tile([P, tiles, 2, P], F32, name="flipped", tag="bank%d" % bank)
+            for j in range(tiles):
                 for h in range(2):
                     every_2nd = slice(j * WORDS + h, (j + 1) * WORDS, 2)
                     nc.tensor.transpose(flipped[:, j, h, :], words[:, every_2nd], identity[:])
             flipped_of[u] = flipped
 
         def copy_out(u):
-            grouped = grouped_pool.tile([P, UNIT * K], BF16, align_bytes=64, name="grouped")
-            dst = grouped[:].bitcast(F32).rearrange("p (j row h) -> p j row h", j=UNIT, h=2)
+            tiles = units[u][0]
+            grouped = grouped_pool.tile([P, tiles * K], BF16, align_bytes=64, name="grouped")
+            dst = grouped[:].bitcast(F32).rearrange("p (j row h) -> p j row h", j=tiles, h=2)
             src = flipped_of[u][:].rearrange("p j h row -> p j row h")
-            if u % VECTOR_COPIES_EVERY == 0:
+            if u % COPY_CYCLE in VECTOR_COPIES:
                 nc.vector.tensor_copy(out=dst, in_=src)
             else:
                 nc.scalar.copy(out=dst, in_=src)
             grouped_of[u] = grouped
 
         def quantise(u):
+            codes, scales = units[u][2:]
             nc.vector.quantize_mx(
-                out=units[u][1].bitcast(FP8X4), scales=units[u][2], in_=grouped_of[u][:]
+                out=codes.bitcast(FP8X4), scales=scales, in_=grouped_of[u][:]
             )
 
         def front(u):

@@ -24,8 +24,8 @@ FLIP_BANKS = 2
 PRODUCT_BANKS = PSUM_BANKS - FLIP_BANKS
 FRONT_LEAD = G_UNITS + 4
 WARM_UPS = 12
-COPY_CYCLE = 5
-VECTOR_COPIES = (1, 3)
+COPY_CYCLE = 3
+VECTOR_COPIES = (2,)
 EPS = 1e-12
 
 FLOPS = 2 * (1024 + 8192) * K * N
@@ -137,7 +137,7 @@ def tile_minerva_pb_kernel(tc, features, ex_features, g_weight, out_0, out_1):
 
         products_of = {}
         result_of = {}
-        floored_of = {}
+        sumsq_of = {}
         inverse_of = {}
 
         def multiply(pair):
@@ -161,7 +161,7 @@ def tile_minerva_pb_kernel(tc, features, ex_features, g_weight, out_0, out_1):
                 result = result_pool.tile([P, STORE_TILES, N], F32, name="result")
                 result_of[pair * UNIT // STORE_TILES] = result
             sumsq = norm_pool.tile([P, UNIT], F32, name="sumsq")
-            floored = norm_pool.tile([P, UNIT], F32, name="floored")
+            sumsq_of[pair] = sumsq
             for j in range(UNIT):
                 t = pair * UNIT + j
                 nc.scalar.activation(
@@ -170,41 +170,40 @@ def tile_minerva_pb_kernel(tc, features, ex_features, g_weight, out_0, out_1):
                     func=ACT.Square,
                     accum_out=sumsq[:, j : j + 1],
                 )
-                if pair == pairs - 1 or j == UNIT - 1:
-                    fresh = slice(j if pair == pairs - 1 else 0, j + 1)
-                    nc.gpsimd.tensor_scalar(
-                        out=floored[:, fresh],
-                        in0=sumsq[:, fresh],
-                        scalar1=EPS * EPS,
-                        scalar2=None,
-                        op0=ALU.max,
-                    )
                 if j == 0 and 0 <= pair - 1:
                     invert(pair - 1)
-            floored_of[pair] = floored
 
         def invert(pair):
             inverse = norm_pool.tile([P, UNIT], F32, name="inverse")
-            width = 1 if pair == pairs - 1 else UNIT
-            for j in range(0, UNIT, width):
-                nc.scalar.activation(
-                    out=inverse[:, j : j + width],
-                    in_=floored_of[pair][:, j : j + width],
-                    func=ACT.Abs_reciprocal_sqrt,
-                )
+            nc.scalar.activation(
+                out=inverse[:], in_=sumsq_of[pair][:], func=ACT.Abs_reciprocal_sqrt
+            )
             inverse_of[pair] = inverse
 
         def scale_and_store(pair):
+            if pair == pairs - 1:
+                capped = norm_pool.tile([P, 1], F32, name="capped")
+                nc.vector.tensor_scalar(
+                    out=capped[:],
+                    in0=inverse_of[pair][:, UNIT - 1 : UNIT],
+                    scalar1=1 / EPS,
+                    scalar2=None,
+                    op0=ALU.min,
+                )
             for j in range(UNIT):
                 t = pair * UNIT + j
                 result = result_of[t // STORE_TILES][:, t % STORE_TILES, :]
                 product = products_of[pair][j][:]
-                inverse = inverse_of[pair][:, j : j + 1]
                 if t == row_tiles - 1:
-                    nc.scalar.activation(out=result, in_=product, func=ACT.Copy, scale=inverse)
+                    nc.scalar.activation(out=result, in_=product, func=ACT.Copy, scale=capped[:])
                 else:
-                    nc.vector.tensor_scalar(
-                        out=result, in0=product, scalar1=inverse, scalar2=None, op0=ALU.mult
+                    nc.vector.scalar_tensor_tensor(
+                        out=result,
+                        in0=inverse_of[pair][:, j : j + 1].to_broadcast([P, N]),
+                        scalar=1 / EPS,
+                        in1=product,
+                        op0=ALU.min,
+                        op1=ALU.mult,
                     )
                 count = 1 if pair == pairs - 1 else STORE_TILES
                 if (t + 1) % count == 0:

@@ -110,12 +110,15 @@ def tile_minerva_pb_kernel(tc, features, ex_features, g_weight, out_0, out_1):
                     nc.tensor.transpose(flipped[:, j, h, :], words[:, every_2nd], identity[:])
             flipped_of[u] = flipped
 
+        def on_vector(u):
+            return u % COPY_CYCLE in VECTOR_COPIES
+
         def copy_out(u):
             tiles = units[u][0]
             grouped = grouped_pool.tile([P, tiles * K], BF16, align_bytes=64, name="grouped")
             dst = grouped[:].bitcast(F32).rearrange("p (j row h) -> p j row h", j=tiles, h=2)
             src = flipped_of[u][:].rearrange("p j h row -> p j row h")
-            if u % COPY_CYCLE in VECTOR_COPIES:
+            if on_vector(u):
                 nc.vector.tensor_copy(out=dst, in_=src)
             else:
                 nc.scalar.copy(out=dst, in_=src)
@@ -156,7 +159,7 @@ def tile_minerva_pb_kernel(tc, features, ex_features, g_weight, out_0, out_1):
                 )
                 products_of[pair].append(acc)
 
-        def inverse_norms(pair):
+        def square_rows(pair):
             if pair * UNIT % STORE_TILES == 0:
                 result = result_pool.tile([P, STORE_TILES, N], F32, name="result")
                 result_of[pair * UNIT // STORE_TILES] = result
@@ -170,7 +173,7 @@ def tile_minerva_pb_kernel(tc, features, ex_features, g_weight, out_0, out_1):
                     func=ACT.Square,
                     accum_out=sumsq[:, j : j + 1],
                 )
-                if j == 0 and 0 <= pair - 1:
+                if j == 0 and 0 <= pair - 1 and pair - 1 not in inverse_of:
                     invert(pair - 1)
 
         def invert(pair):
@@ -181,7 +184,8 @@ def tile_minerva_pb_kernel(tc, features, ex_features, g_weight, out_0, out_1):
             inverse_of[pair] = inverse
 
         def scale_and_store(pair):
-            if pair == pairs - 1:
+            ending = pair >= pairs - 2
+            if ending:
                 capped = norm_pool.tile([P, 1], F32, name="capped")
                 nc.vector.tensor_scalar(
                     out=capped[:],
@@ -194,9 +198,13 @@ def tile_minerva_pb_kernel(tc, features, ex_features, g_weight, out_0, out_1):
                 t = pair * UNIT + j
                 result = result_of[t // STORE_TILES][:, t % STORE_TILES, :]
                 product = products_of[pair][j][:]
-                if t == row_tiles - 1:
-                    nc.scalar.activation(out=result, in_=product, func=ACT.Copy, scale=capped[:])
+                if not ending:
+                    parts = []
+                elif t < row_tiles - 1:
+                    parts = [slice(0, N)]
                 else:
+                    parts = [slice(0, N // 2), slice(N // 2, N)]
+                if not (ending and j == UNIT - 1):
                     nc.vector.scalar_tensor_tensor(
                         out=result,
                         in0=inverse_of[pair][:, j : j + 1].to_broadcast([P, N]),
@@ -205,15 +213,20 @@ def tile_minerva_pb_kernel(tc, features, ex_features, g_weight, out_0, out_1):
                         op0=ALU.min,
                         op1=ALU.mult,
                     )
-                count = 1 if pair == pairs - 1 else STORE_TILES
-                if (t + 1) % count == 0:
-                    first = t + 1 - count
+                for cols in parts:
+                    if j == UNIT - 1:
+                        nc.scalar.activation(
+                            out=result[:, cols], in_=product[:, cols], func=ACT.Copy, scale=capped[:]
+                        )
                     nc.sync.dma_start(
-                        out=out_views[first // GROUP][:, first % GROUP : first % GROUP + count, :],
-                        in_=result_of[first // STORE_TILES][
-                            :, first % STORE_TILES : first % STORE_TILES + count, :
-                        ],
+                        out=out_views[t // GROUP][:, t % GROUP, cols], in_=result[:, cols]
                     )
+            if not ending:
+                first = pair * UNIT
+                nc.sync.dma_start(
+                    out=out_views[first // GROUP][:, first % GROUP : first % GROUP + UNIT, :],
+                    in_=result_of[first // STORE_TILES][:],
+                )
 
         for u in range(FRONT_LEAD):
             front(u)
@@ -221,9 +234,12 @@ def tile_minerva_pb_kernel(tc, features, ex_features, g_weight, out_0, out_1):
             if i < pairs:
                 multiply(i)
             if 0 <= i - 1 < pairs:
-                inverse_norms(i - 1)
-            if i - 1 == pairs:
+                square_rows(i - 1)
+            if i == pairs:
                 invert(pairs - 1)
             if 0 <= i - 2:
                 scale_and_store(i - 2)
-            front(FRONT_LEAD + i)
+            u = FRONT_LEAD + i
+            front(u)
+            if 0 <= i - 1 and u - 1 < len(units) and not on_vector(u - 1):
+                invert(i - 1)

@@ -24,7 +24,7 @@ FLIP_BANKS = 2
 PRODUCT_BANKS = PSUM_BANKS - FLIP_BANKS
 FRONT_LEAD = G_UNITS + 4
 WARM_UPS = 12
-COPY_CYCLE = 3
+COPY_CYCLE = 4
 VECTOR_COPIES = (2,)
 EPS = 1e-12
 
@@ -38,8 +38,8 @@ def tile_minerva_pb_kernel(tc, features, ex_features, g_weight, out_0, out_1):
     with ExitStack() as ctx:
         const = ctx.enter_context(tc.tile_pool(name="const", bufs=1))
         rows_pool = ctx.enter_context(tc.tile_pool(name="rows", bufs=1))
-        grouped_pool = ctx.enter_context(tc.tile_pool(name="grouped", bufs=3))
-        norm_pool = ctx.enter_context(tc.tile_pool(name="norms", bufs=3))
+        grouped_pool = ctx.enter_context(tc.tile_pool(name="grouped", bufs=4))
+        norm_pool = ctx.enter_context(tc.tile_pool(name="norms", bufs=4))
         result_pool = ctx.enter_context(tc.tile_pool(name="result", bufs=16))
         psum = ctx.enter_context(tc.psum_pool(name="psum", bufs=1))
         ctx.enter_context(tc.manual_schedule())
@@ -129,14 +129,6 @@ def tile_minerva_pb_kernel(tc, features, ex_features, g_weight, out_0, out_1):
             nc.vector.quantize_mx(
                 out=codes.bitcast(FP8X4), scales=scales, in_=grouped_of[u][:]
             )
-
-        def front(u):
-            if u < len(units):
-                transpose(u)
-            if 0 <= u - 1 < len(units):
-                copy_out(u - 1)
-            if 0 <= u - 2 < len(units):
-                quantise(u - 2)
 
         products_of = {}
         result_of = {}
@@ -228,18 +220,33 @@ def tile_minerva_pb_kernel(tc, features, ex_features, g_weight, out_0, out_1):
                     in_=result_of[first // STORE_TILES][:],
                 )
 
-        for u in range(FRONT_LEAD):
-            front(u)
-        for i in range(pairs + 2):
-            if i < pairs:
-                multiply(i)
-            if 0 <= i - 1 < pairs:
-                square_rows(i - 1)
-            if i == pairs:
+        for u in range(FRONT_LEAD + 1):
+            transpose(u)
+            if 1 <= u < FRONT_LEAD:
+                copy_out(u - 1)
+            if u >= 2:
+                quantise(u - 2)
+
+        for a in range(0, pairs + 1, 2):
+            u = FRONT_LEAD + a
+            if a == pairs:
                 invert(pairs - 1)
-            if 0 <= i - 2:
-                scale_and_store(i - 2)
-            u = FRONT_LEAD + i
-            front(u)
-            if 0 <= i - 1 and u - 1 < len(units) and not on_vector(u - 1):
-                invert(i - 1)
+            if a < pairs:
+                multiply(a)
+            if a >= 2:
+                scale_and_store(a - 2)
+            for v in (u - 1, u):
+                if v < len(units):
+                    copy_out(v)
+            if a < pairs:
+                square_rows(a)
+                multiply(a + 1)
+                square_rows(a + 1)
+            for v in (u + 1, u + 2):
+                if v < len(units):
+                    transpose(v)
+            for v in (u - 1, u):
+                if v < len(units):
+                    quantise(v)
+            if a >= 1:
+                scale_and_store(a - 1)

from contextlib import ExitStack

import concourse.mybir as mybir
from concourse.masks import make_identity

F32 = mybir.dt.float32
BF16 = mybir.dt.bfloat16
U32 = mybir.dt.uint32
U8 = mybir.dt.uint8
FP8X4 = mybir.dt.float8_e4m3fn_x4
ACT = mybir.ActivationFunctionType
ALU = mybir.AluOpType

P = 128
K = 512
N = 512
WORDS = K // 2
UNIT = 2
G_UNITS = N // P
GROUP = 8
STORE_TILES = 2
PSUM_BANKS = 8
FLIP_BANKS = 2
PRODUCT_BANKS = PSUM_BANKS - FLIP_BANKS
FRONT_LEAD = G_UNITS + 4
WARM_UPS = 12
COPY_CYCLE = 4
VECTOR_COPIES = (2,)
EPS = 1e-12

FLOPS = 2 * (1024 + 8192) * K * N


def tile_minerva_pb_kernel(tc, features, ex_features, g_weight, out_0, out_1):
    nc = tc.nc
    row_tiles = (features.shape[0] + ex_features.shape[0]) // P
    pairs = row_tiles // UNIT
    with ExitStack() as ctx:
        const = ctx.enter_context(tc.tile_pool(name="const", bufs=1))
        rows_pool = ctx.enter_context(tc.tile_pool(name="rows", bufs=1))
        grouped_pool = ctx.enter_context(tc.tile_pool(name="grouped", bufs=4))
        norm_pool = ctx.enter_context(tc.tile_pool(name="norms", bufs=4))
        result_pool = ctx.enter_context(tc.tile_pool(name="result", bufs=16))
        psum = ctx.enter_context(tc.psum_pool(name="psum", bufs=1))
        ctx.enter_context(tc.manual_schedule())

        g_rows = const.tile([P, G_UNITS * K], BF16, name="g_rows")
        g_src = g_weight.rearrange("(t p) k -> p t k", p=P)
        for b in range(G_UNITS):
            nc.sync.dma_start(out=g_rows[:, b * K : (b + 1) * K], in_=g_src[:, b, :])
        x_words = []
        out_views = []
        for x, out in ((features, out_0), (ex_features, out_1)):
            for base in range(0, x.shape[0], GROUP * P):
                x_rows = rows_pool.tile([P, GROUP * K], BF16, name="x_rows%d" % len(out_views))
                src = x[base : base + GROUP * P, :].rearrange("(p t) k -> p (t k)", t=GROUP)
                pieces = GROUP // UNIT if len(out_views) < 2 else 1
                width = GROUP * K // pieces
                for c in range(pieces):
                    cols = slice(c * width, (c + 1) * width)
                    nc.sync.dma_start(out=x_rows[:, cols], in_=src[:, cols])
                words = x_rows[:].bitcast(F32)
                for c in range(GROUP // UNIT):
                    x_words.append(words[:, c * UNIT * WORDS : (c + 1) * UNIT * WORDS])
                out_views.append(
                    out[base : base + GROUP * P, :].rearrange("(p t) n -> p t n", t=GROUP)
                )

        zeros = const.tile([P, P], BF16, name="zeros")
        nc.vector.memset(zeros[:], 0.0)
        idle = psum.tile([P, P], F32, name="idle", tag="bank%d" % (PSUM_BANKS - 1))
        for turn in range(WARM_UPS):
            nc.tensor.matmul(
                idle[:], lhsT=zeros[:], rhs=zeros[:], start=turn == 0, stop=turn == WARM_UPS - 1
            )

        one = const.tile([P, 1], F32, name="one")
        nc.vector.memset(one[:], 1.0)
        table_loaded = const.tile([P, 1], F32, name="table_loaded")
        nc.scalar.activation(out=table_loaded[:], in_=one[:], func=ACT.Abs_reciprocal_sqrt)

        identity = const.tile([P, P], F32, name="identity")
        make_identity(nc, identity[:])

        g_codes = const.tile([P, N], U32, align_bytes=64, name="g_codes")
        g_scales = const.tile([P, N], U8, align_bytes=64, name="g_scales")
        x_codes = const.tile([P, row_tiles * P], U32, align_bytes=64, name="x_codes")
        x_scales = const.tile([P, row_tiles * P], U8, align_bytes=64, name="x_scales")

        g_words = g_rows[:].bitcast(F32)
        units = []
        for b in range(G_UNITS):
            cols = slice(b * P, (b + 1) * P)
            words = g_words[:, b * WORDS : (b + 1) * WORDS]
            units.append((1, words, g_codes[:, cols], g_scales[:, cols]))
        for pair in range(pairs):
            cols = slice(pair * UNIT * P, (pair + 1) * UNIT * P)
            units.append((UNIT, x_words[pair], x_codes[:, cols], x_scales[:, cols]))

        flipped_of = {}
        grouped_of = {}

        def transpose(u):
            bank = u if u < PRODUCT_BANKS else PRODUCT_BANKS + u % FLIP_BANKS
            tiles, words = units[u][:2]
            flipped = psum.tile([P, tiles, 2, P], F32, name="flipped", tag="bank%d" % bank)
            for j in range(tiles):
                for h in range(2):
                    every_2nd = slice(j * WORDS + h, (j + 1) * WORDS, 2)
                    nc.tensor.transpose(flipped[:, j, h, :], words[:, every_2nd], identity[:])
            flipped_of[u] = flipped

        def on_vector(u):
            return u % COPY_CYCLE in VECTOR_COPIES

        def copy_out(u):
            tiles = units[u][0]
            grouped = grouped_pool.tile([P, tiles * K], BF16, align_bytes=64, name="grouped")
            dst = grouped[:].bitcast(F32).rearrange("p (j row h) -> p j row h", j=tiles, h=2)
            src = flipped_of[u][:].rearrange("p j h row -> p j row h")
            if on_vector(u):
                nc.vector.tensor_copy(out=dst, in_=src)
            else:
                nc.scalar.copy(out=dst, in_=src)
            grouped_of[u] = grouped

        def quantise(u):
            codes, scales = units[u][2:]
            nc.vector.quantize_mx(
                out=codes.bitcast(FP8X4), scales=scales, in_=grouped_of[u][:]
            )

        products_of = {}
        result_of = {}
        sumsq_of = {}
        inverse_of = {}

        def multiply(pair):
            products_of[pair] = []
            for j in range(UNIT):
                t = pair * UNIT + j
                acc = psum.tile([P, N], F32, name="acc", tag="bank%d" % (t % PRODUCT_BANKS))
                nc.tensor.matmul_mx(
                    out=acc[:],
                    lhsT=x_codes[:, t * P : (t + 1) * P].bitcast(FP8X4),
                    lhsT_scale=x_scales[:, t * P : (t + 1) * P],
                    rhs=g_codes[:].bitcast(FP8X4),
                    rhs_scale=g_scales[:],
                    start=True,
                    stop=True,
                )
                products_of[pair].append(acc)

        def square_rows(pair):
            if pair * UNIT % STORE_TILES == 0:
                result = result_pool.tile([P, STORE_TILES, N], F32, name="result")
                result_of[pair * UNIT // STORE_TILES] = result
            sumsq = norm_pool.tile([P, UNIT], F32, name="sumsq")
            sumsq_of[pair] = sumsq
            for j in range(UNIT):
                t = pair * UNIT + j
                nc.scalar.activation(
                    out=result_of[t // STORE_TILES][:, t % STORE_TILES, :],
                    in_=products_of[pair][j][:],
                    func=ACT.Square,
                    accum_out=sumsq[:, j : j + 1],
                )
                if j == 0 and 0 <= pair - 1 and pair - 1 not in inverse_of:
                    invert(pair - 1)

        def invert(pair):
            inverse = norm_pool.tile([P, UNIT], F32, name="inverse")
            nc.scalar.activation(
                out=inverse[:], in_=sumsq_of[pair][:], func=ACT.Abs_reciprocal_sqrt
            )
            inverse_of[pair] = inverse

        def scale_and_store(pair):
            ending = pair >= pairs - 2
            if ending:
                capped = norm_pool.tile([P, 1], F32, name="capped")
                nc.vector.tensor_scalar(
                    out=capped[:],
                    in0=inverse_of[pair][:, UNIT - 1 : UNIT],
                    scalar1=1 / EPS,
                    scalar2=None,
                    op0=ALU.min,
                )
            for j in range(UNIT):
                t = pair * UNIT + j
                result = result_of[t // STORE_TILES][:, t % STORE_TILES, :]
                product = products_of[pair][j][:]
                if not ending:
                    parts = []
                elif t < row_tiles - 1:
                    parts = [slice(0, N)]
                else:
                    parts = [slice(0, N // 2), slice(N // 2, N)]
                if not (ending and j == UNIT - 1):
                    nc.vector.scalar_tensor_tensor(
                        out=result,
                        in0=inverse_of[pair][:, j : j + 1].to_broadcast([P, N]),
                        scalar=1 / EPS,
                        in1=product,
                        op0=ALU.min,
                        op1=ALU.mult,
                    )
                for cols in parts:
                    if j == UNIT - 1:
                        nc.scalar.activation(
                            out=result[:, cols], in_=product[:, cols], func=ACT.Copy, scale=capped[:]
                        )
                    nc.sync.dma_start(
                        out=out_views[t // GROUP][:, t % GROUP, cols], in_=result[:, cols]
                    )
            if not ending:
                first = pair * UNIT
                nc.sync.dma_start(
                    out=out_views[first // GROUP][:, first % GROUP : first % GROUP + UNIT, :],
                    in_=result_of[first // STORE_TILES][:],
                )

        for u in range(FRONT_LEAD + 1):
            transpose(u)
            if 1 <= u < FRONT_LEAD:
                copy_out(u - 1)
            if u >= 2:
                quantise(u - 2)

        for a in range(0, pairs + 1, 2):
            u = FRONT_LEAD + a
            if a == pairs:
                invert(pairs - 1)
            if a < pairs:
                multiply(a)
            if a >= 2:
                scale_and_store(a - 2)
            for v in (u - 1, u):
                if v < len(units):
                    copy_out(v)
            if a < pairs:
                square_rows(a)
                multiply(a + 1)
                square_rows(a + 1)
            for v in (u + 1, u + 2):
                if v < len(units):
                    transpose(v)
            for v in (u - 1, u):
                if v < len(units):
                    quantise(v)
            if a >= 1:
                scale_and_store(a - 1)
